import numpy as np
import ml_dtypes


def mxq(x, axis, fmt="e4m3"):
    dtype, down = {"e4m3": (ml_dtypes.float8_e4m3fn, 7), "e5m2": (ml_dtypes.float8_e5m2, 14)}[fmt]
    v = np.moveaxis(np.asarray(x, np.float32).astype(ml_dtypes.bfloat16).astype(np.float64), axis, -1)
    blocks = v.reshape(v.shape[:-1] + (-1, 32))
    amax = np.abs(blocks).max(-1, keepdims=True)
    byte = np.maximum(np.where(amax > 0, np.frexp(amax)[1] - 1 + 127, 0) - down, 1)
    scale = np.exp2(byte - 127.0)
    codes = (blocks / scale).astype(np.float32).astype(dtype).astype(np.float64)
    return np.moveaxis((codes * scale).reshape(v.shape), -1, axis)


WIDE = False


def mx_kscale(k):
    if not WIDE:
        return np.ones(k)
    levels = np.array([10, -10, 5, -5, 0])
    a = np.random.permutation(np.resize(levels, k // 512 * 4)).reshape(k // 512, 4)
    idx = np.arange(k)
    return np.exp2(a[idx // 512, idx % 128 // 32])


BF16 = ml_dtypes.bfloat16


def bf(x):
    return np.asarray(x, np.float32).astype(BF16)


def f64(x):
    return np.asarray(x).astype(np.float64)


B, L, D, E, S = 8, 1024, 1024, 64, 128
F = E + E + S
LN_EPS = 1e-5
GQ = 1.75 * np.sqrt(np.sqrt(10.0 * L / S))


def silu(v):
    return v / (1.0 + np.exp(-v))


def setup_inputs():
    n = np.random.standard_normal
    s = mx_kscale(D)
    return {"x": bf(0.7 * n((B, L, D)) + 0.3 * n((B, L, 1))),
            "ln_g": bf((1.0 + 0.1 * n(D)) * s),
            "ln_b": bf(0.1 * n(D) * s),
            "W_in": bf(n((D, F)) / np.sqrt(D) / s[:, None]),
            "b_in": bf(0.2 * n(F)),
            "gamma_q": bf(GQ * (1.0 + 0.1 * n(S))),
            "beta_q": bf(GQ * (-0.2 + 0.1 * n(S))),
            "gamma_k": bf(GQ * (1.0 + 0.1 * n(S))),
            "beta_k": bf(GQ * (-0.2 + 0.1 * n(S)))}


def reference(x, ln_g, ln_b, W_in, b_in, gamma_q, beta_q, gamma_k, beta_k):
    x = f64(x)
    mu = x.mean(-1, keepdims=True)
    var = np.square(x - mu).mean(-1, keepdims=True)
    xn = (x - mu) / np.sqrt(var + LN_EPS) * f64(ln_g) + f64(ln_b)
    uvz = silu((mxq(xn, 2, "e4m3") @ mxq(f64(W_in), 0, "e4m3")) + f64(b_in))
    u, v, z = uvz[..., :E], uvz[..., E:E + E], uvz[..., E + E:]
    q = z * f64(gamma_q) + f64(beta_q)
    k = z * f64(gamma_k) + f64(beta_k)
    return u, v, q, k

@@ -1,0 +1,281 @@
+from contextlib import ExitStack
+
+import concourse.mybir as mybir
+from concourse.masks import make_identity
+
+F32 = mybir.dt.float32
+BF16 = mybir.dt.bfloat16
+U32 = mybir.dt.uint32
+U8 = mybir.dt.uint8
+FP8X4 = mybir.dt.float8_e4m3fn_x4
+ACT = mybir.ActivationFunctionType
+ALU = mybir.AluOpType
+
+P = 128
+ROWS = 8192
+D = 1024
+F = 256
+E = 64
+S = 128
+LN_EPS = 1e-5
+TG = 4
+GROUP = TG * P
+NG = ROWS // GROUP
+PASSES = D // 512
+FLOPS = 2 * ROWS * D * F
+
+XHAT_ENGINE = ("g", "g", "g", "s")
+LOAD_AHEAD = 4
+STAT_AHEAD = 3
+XHAT_AHEAD = 2
+
+
+def tile_gaublock_pb_t_kernel(
+    tc, x, ln_g, ln_b, W_in, b_in, gamma_q, beta_q, gamma_k, beta_k, out_0, out_1, out_2, out_3
+):
+    nc = tc.nc
+    xf = x.flatten_outer_dims()
+    outs = (
+        out_0.flatten_outer_dims(),
+        out_1.flatten_outer_dims(),
+        out_2.flatten_outer_dims(),
+        out_3.flatten_outer_dims(),
+    )
+
+    with ExitStack() as ctx:
+        const = ctx.enter_context(tc.tile_pool(name="const", bufs=1))
+        xpool = ctx.enter_context(tc.tile_pool(name="xpool", bufs=LOAD_AHEAD))
+        small = ctx.enter_context(tc.tile_pool(name="small", bufs=4))
+        xhpool = ctx.enter_context(tc.tile_pool(name="xhpool", bufs=2))
+        work = ctx.enter_context(tc.tile_pool(name="work", bufs=2))
+        outp = ctx.enter_context(tc.tile_pool(name="outp", bufs=3))
+        psT = ctx.enter_context(tc.psum_pool(name="psT", bufs=4))
+        psM = ctx.enter_context(tc.psum_pool(name="psM", bufs=2))
+        psO = ctx.enter_context(tc.psum_pool(name="psO", bufs=2))
+        ctx.enter_context(tc.manual_schedule())
+
+        tiles = {}
+
+        def load(g):
+            xt = xpool.tile([P, TG, D], BF16, name="xt")
+            tiles[("x", g)] = xt
+            src = xf[g * GROUP : (g + 1) * GROUP, :].rearrange("(p t) k -> p t k", t=TG)
+            if g == 0:
+                for t in range(TG):
+                    nc.sync.dma_start(out=xt[:, t, :], in_=src[:, t, :])
+            else:
+                nc.sync.dma_start(out=xt[:], in_=src)
+
+        load(0)
+        ident = const.tile([P, P], F32)
+        make_identity(nc, ident[:])
+        mhalf = const.tile([P, TG], F32)
+        nc.vector.memset(mhalf[:], -0.5)
+        prm_bf = const.tile([P, P], BF16)
+        nc.vector.memset(prm_bf[:], 0.0)
+        nc.scalar.dma_start(out=prm_bf[0:8, :], in_=ln_g.rearrange("(j p) -> j p", p=P))
+        nc.scalar.dma_start(out=prm_bf[8:16, :], in_=ln_b.rearrange("(j p) -> j p", p=P))
+        nc.scalar.dma_start(out=prm_bf[16:18, :], in_=b_in.rearrange("(j p) -> j p", p=P))
+        nc.scalar.dma_start(out=prm_bf[18:19, :], in_=gamma_q.rearrange("(j p) -> j p", p=P))
+        nc.scalar.dma_start(out=prm_bf[19:20, :], in_=beta_q.rearrange("(j p) -> j p", p=P))
+        nc.scalar.dma_start(out=prm_bf[20:21, :], in_=gamma_k.rearrange("(j p) -> j p", p=P))
+        nc.scalar.dma_start(out=prm_bf[21:22, :], in_=beta_k.rearrange("(j p) -> j p", p=P))
+        load(1)
+        wraw = const.tile([P, PASSES * 4, F], BF16)
+        nc.sync.dma_start(out=wraw[:], in_=W_in.rearrange("(j p) f -> p j f", p=P))
+        for g in range(2, LOAD_AHEAD):
+            load(g)
+
+        prm = const.tile([P, 32], F32)
+        wcodes = const.tile([P, PASSES * F], U32, align_bytes=64)
+        wsc = const.tile([P, PASSES * F], U8, align_bytes=64)
+
+        def prepare_params():
+            prm_f = const.tile([P, P], F32)
+            nc.vector.tensor_copy(out=prm_f[:], in_=prm_bf[:])
+            prm_ps = psO.tile([P, 512], F32, tag="bo", name="prm_ps")
+            nc.tensor.transpose(out=prm_ps[:, 0:P], in_=prm_f[:], identity=ident[:])
+            nc.vector.tensor_copy(out=prm[:], in_=prm_ps[:, 0:32])
+
+        def prepare_w():
+            wgrp = const.tile([P, PASSES, F, 4], BF16, align_bytes=64)
+            nc.vector.tensor_copy(out=wgrp[:], in_=wraw[:].rearrange("p (c t) f -> p c f t", t=4))
+            nc.vector.quantize_mx(
+                out=wcodes[:].bitcast(FP8X4),
+                scales=wsc[:],
+                in_=wgrp[:].rearrange("p c f t -> p (c f t)"),
+            )
+
+        def stats(g):
+            xt = tiles[("x", g)]
+            st = small.tile([P, TG, 2, 6], F32, name="st")
+            mv = small.tile([P, TG, 2], F32, name="mv")
+            for t in range(TG):
+                for h in range(2):
+                    nc.vector.bn_stats(out=st[:, t, h, :], in_=xt[:, t, h * 512 : (h + 1) * 512])
+                nc.vector.bn_aggr(out=mv[:, t, :], in_=st[:, t, :, :].rearrange("p h s -> p (h s)"))
+            negmu = small.tile([P, TG], F32, name="negmu")
+            ve = small.tile([P, TG], F32, name="ve")
+            rstd = small.tile([P, TG], F32, name="rstd")
+            nc.vector.tensor_scalar(out=negmu[:], in0=mv[:, :, 0], scalar1=-1.0, scalar2=None, op0=ALU.mult)
+            nc.vector.tensor_scalar(out=ve[:], in0=mv[:, :, 1], scalar1=LN_EPS, scalar2=None, op0=ALU.add)
+            nc.gpsimd.tensor_tensor(out=rstd[:], in0=ve[:], in1=mhalf[:], op=ALU.pow)
+            tiles[("negmu", g)] = negmu
+            tiles[("rstd", g)] = rstd
+
+        def xhat_prepare(g):
+            nmr = small.tile([P, TG], F32, name="nmr")
+            nc.vector.tensor_tensor(out=nmr[:], in0=tiles[("negmu", g)][:], in1=tiles[("rstd", g)][:], op=ALU.mult)
+            tiles[("nmr", g)] = nmr
+            tiles[("xh", g)] = xhpool.tile([P, TG, D], F32, name="xh")
+
+        def xhat(g, t):
+            xt = tiles[("x", g)]
+            xh = tiles[("xh", g)]
+            e = XHAT_ENGINE[t]
+            if e == "s":
+                nc.scalar.activation(
+                    out=xh[:, t, :], in_=xt[:, t, :], func=ACT.Identity,
+                    bias=tiles[("nmr", g)][:, t : t + 1], scale=tiles[("rstd", g)][:, t : t + 1],
+                )
+            else:
+                eng = nc.gpsimd if e == "g" else nc.vector
+                eng.tensor_scalar(
+                    out=xh[:, t, :], in0=xt[:, t, :],
+                    scalar1=tiles[("negmu", g)][:, t : t + 1], scalar2=tiles[("rstd", g)][:, t : t + 1],
+                    op0=ALU.add, op1=ALU.mult,
+                )
+
+        def turn(g, j):
+            if j == 0:
+                tiles[("planes", g)] = work.tile([P, PASSES, 4, GROUP], BF16, name="planes")
+            xh = tiles[("xh", g)]
+            bank = psT.tile([P, GROUP], F32, name="bank")
+            for t in range(TG):
+                nc.tensor.transpose(
+                    out=bank[:, t * P : (t + 1) * P], in_=xh[:, t, j * P : (j + 1) * P], identity=ident[:]
+                )
+            nc.scalar.activation(
+                out=tiles[("planes", g)][:, j // 4, j % 4, :], in_=bank[:], func=ACT.Identity,
+                bias=prm[:, 8 + j : 9 + j], scale=prm[:, j : j + 1],
+            )
+
+        def quantise(g):
+            planes = tiles[("planes", g)]
+            grouped = work.tile([P, PASSES, GROUP, 4], BF16, align_bytes=64, name="grouped")
+            for c in range(PASSES):
+                nc.vector.tensor_copy(
+                    out=grouped[:, c].rearrange("p (w i) t -> p w t i", i=4),
+                    in_=planes[:, c].rearrange("p t (w i) -> p w t i", i=4),
+                )
+            codes = work.tile([P, PASSES * GROUP], U32, align_bytes=64, name="codes")
+            sc = work.tile([P, PASSES * GROUP], U8, align_bytes=64, name="sc")
+            nc.vector.quantize_mx(
+                out=codes[:].bitcast(FP8X4), scales=sc[:], in_=grouped[:].rearrange("p c n t -> p (c n t)")
+            )
+            tiles[("codes", g)] = codes
+            tiles[("sc", g)] = sc
+
+        def multiply(g):
+            codes = tiles[("codes", g)]
+            sc = tiles[("sc", g)]
+            sil = work.tile([P, 2, GROUP], F32, name="sil")
+            tiles[("sil", g)] = sil
+            accs = []
+            for h in range(2):
+                acc = psM.tile([P, GROUP], F32, name="acc")
+                accs.append(acc)
+                for c in range(PASSES):
+                    w0 = c * F + h * P
+                    nc.tensor.matmul_mx(
+                        out=acc[:],
+                        lhsT=wcodes[:, w0 : w0 + P].bitcast(FP8X4),
+                        lhsT_scale=wsc[:, w0 : w0 + P],
+                        rhs=codes[:, c * GROUP : (c + 1) * GROUP].bitcast(FP8X4),
+                        rhs_scale=sc[:, c * GROUP : (c + 1) * GROUP],
+                        start=(c == 0),
+                        stop=(c == PASSES - 1),
+                    )
+            for h in range(2):
+                nc.scalar.activation(
+                    out=sil[:, h, :], in_=accs[h][:], func=ACT.Silu, bias=prm[:, 16 + h : 17 + h], scale=1.0
+                )
+
+        def scale_offset(g):
+            sil = tiles[("sil", g)]
+            qk = work.tile([P, 2, GROUP], F32, name="qk")
+            tiles[("qk", g)] = qk
+            for i in range(2):
+                nc.vector.tensor_scalar(
+                    out=qk[:, i, :], in0=sil[:, 1, :],
+                    scalar1=prm[:, 18 + 2 * i : 19 + 2 * i], scalar2=prm[:, 19 + 2 * i : 20 + 2 * i],
+                    op0=ALU.mult, op1=ALU.add,
+                )
+
+        def emit_out(g, i):
+            src = tiles[("sil", g)][:, 0, :] if i == 0 else tiles[("qk", g)][:, i - 1, :]
+            rows = slice(g * GROUP, (g + 1) * GROUP)
+            bo = psO.tile([P, 512], F32, tag="bo", name="bo")
+            for t in range(TG):
+                nc.tensor.transpose(
+                    out=bo[:, t * P : (t + 1) * P], in_=src[:, t * P : (t + 1) * P], identity=ident[:]
+                )
+            if i == 0:
+                st_uv = outp.tile([P, 2, TG, E], F32, name="st_uv")
+                nc.scalar.copy(
+                    out=st_uv[:].rearrange("p c t f -> p t c f"),
+                    in_=bo[:].rearrange("p (t c f) -> p t c f", t=TG, c=2),
+                )
+                for c in range(2):
+                    nc.sync.dma_start(
+                        out=outs[c][rows, :].rearrange("(p t) f -> p (t f)", t=TG),
+                        in_=st_uv[:, c].rearrange("p t f -> p (t f)"),
+                    )
+            else:
+                st_o = outp.tile([P, TG * S], F32, name="st_o", bufs=6)
+                nc.scalar.copy(out=st_o[:], in_=bo[:])
+                nc.sync.dma_start(
+                    out=outs[1 + i][rows, :].rearrange("(p t) f -> p (t f)", t=TG), in_=st_o[:]
+                )
+
+        def live(g):
+            return 0 <= g < NG
+
+        for i in range(-STAT_AHEAD, NG):
+            if i >= 0 and live(i + LOAD_AHEAD):
+                load(i + LOAD_AHEAD)
+            gx = i + XHAT_AHEAD
+            gs = i + STAT_AHEAD
+            if live(gx):
+                xhat_prepare(gx)
+                for t in range(TG):
+                    if XHAT_ENGINE[t] != "s":
+                        xhat(gx, t)
+            if live(i + 1):
+                turn(i + 1, 0)
+                turn(i + 1, 1)
+            if live(i):
+                multiply(i)
+            if live(i + 1):
+                turn(i + 1, 2)
+            if live(i):
+                emit_out(i, 0)
+            if live(i + 1):
+                for j in range(3, 8):
+                    turn(i + 1, j)
+            if live(gs):
+                stats(gs)
+            if gs == 0:
+                prepare_params()
+            if gs == 1:
+                prepare_w()
+            if live(gx):
+                for t in range(TG):
+                    if XHAT_ENGINE[t] == "s":
+                        xhat(gx, t)
+            if live(i):
+                scale_offset(i)
+                emit_out(i, 1)
+                emit_out(i, 2)
+            if live(i + 1):
+                quantise(i + 1)

@@ -49,9 +49,9 @@ def tile_gaublock_pb_t_kernel(
         xhpool = ctx.enter_context(tc.tile_pool(name="xhpool", bufs=2))
         work = ctx.enter_context(tc.tile_pool(name="work", bufs=2))
         outp = ctx.enter_context(tc.tile_pool(name="outp", bufs=3))
-        psT = ctx.enter_context(tc.psum_pool(name="psT", bufs=4))
+        psT = ctx.enter_context(tc.psum_pool(name="psT", bufs=3))
         psM = ctx.enter_context(tc.psum_pool(name="psM", bufs=2))
-        psO = ctx.enter_context(tc.psum_pool(name="psO", bufs=2))
+        psO = ctx.enter_context(tc.psum_pool(name="psO", bufs=3))
         ctx.enter_context(tc.manual_schedule())
 
         tiles = {}
@@ -241,41 +241,35 @@ def tile_gaublock_pb_t_kernel(
         def live(g):
             return 0 <= g < NG
 
-        for i in range(-STAT_AHEAD, NG):
+        for i in range(-STAT_AHEAD, NG + 1):
             if i >= 0 and live(i + LOAD_AHEAD):
                 load(i + LOAD_AHEAD)
             gx = i + XHAT_AHEAD
             gs = i + STAT_AHEAD
+            if live(i):
+                quantise(i)
+            if live(i - 1):
+                scale_offset(i - 1)
             if live(gx):
                 xhat_prepare(gx)
                 for t in range(TG):
                     if XHAT_ENGINE[t] != "s":
                         xhat(gx, t)
             if live(i + 1):
-                turn(i + 1, 0)
-                turn(i + 1, 1)
+                for j in range(8):
+                    turn(i + 1, j)
+            if live(gx):
+                for t in range(TG):
+                    if XHAT_ENGINE[t] == "s":
+                        xhat(gx, t)
             if live(i):
                 multiply(i)
-            if live(i + 1):
-                turn(i + 1, 2)
-            if live(i):
-                emit_out(i, 0)
-            if live(i + 1):
-                for j in range(3, 8):
-                    turn(i + 1, j)
+            if live(i - 1):
+                for k in range(3):
+                    emit_out(i - 1, k)
             if live(gs):
                 stats(gs)
             if gs == 0:
                 prepare_params()
             if gs == 1:
                 prepare_w()
-            if live(gx):
-                for t in range(TG):
-                    if XHAT_ENGINE[t] == "s":
-                        xhat(gx, t)
-            if live(i):
-                scale_offset(i)
-                emit_out(i, 1)
-                emit_out(i, 2)
-            if live(i + 1):
-                quantise(i + 1)

@@ -49,9 +49,8 @@ def tile_gaublock_pb_t_kernel(
         xhpool = ctx.enter_context(tc.tile_pool(name="xhpool", bufs=2))
         work = ctx.enter_context(tc.tile_pool(name="work", bufs=2))
         outp = ctx.enter_context(tc.tile_pool(name="outp", bufs=3))
-        psT = ctx.enter_context(tc.psum_pool(name="psT", bufs=3))
+        psT = ctx.enter_context(tc.psum_pool(name="psT", bufs=6))
         psM = ctx.enter_context(tc.psum_pool(name="psM", bufs=2))
-        psO = ctx.enter_context(tc.psum_pool(name="psO", bufs=3))
         ctx.enter_context(tc.manual_schedule())
 
         tiles = {}
@@ -93,7 +92,7 @@ def tile_gaublock_pb_t_kernel(
         def prepare_params():
             prm_f = const.tile([P, P], F32)
             nc.vector.tensor_copy(out=prm_f[:], in_=prm_bf[:])
-            prm_ps = psO.tile([P, 512], F32, tag="bo", name="prm_ps")
+            prm_ps = psT.tile([P, 512], F32, tag="bank", name="prm_ps")
             nc.tensor.transpose(out=prm_ps[:, 0:P], in_=prm_f[:], identity=ident[:])
             nc.vector.tensor_copy(out=prm[:], in_=prm_ps[:, 0:32])
 
@@ -150,7 +149,7 @@ def tile_gaublock_pb_t_kernel(
             if j == 0:
                 tiles[("planes", g)] = work.tile([P, PASSES, 4, GROUP], BF16, name="planes")
             xh = tiles[("xh", g)]
-            bank = psT.tile([P, GROUP], F32, name="bank")
+            bank = psT.tile([P, GROUP], F32, tag="bank", name="bank")
             for t in range(TG):
                 nc.tensor.transpose(
                     out=bank[:, t * P : (t + 1) * P], in_=xh[:, t, j * P : (j + 1) * P], identity=ident[:]
@@ -215,7 +214,7 @@ def tile_gaublock_pb_t_kernel(
         def emit_out(g, i):
             src = tiles[("sil", g)][:, 0, :] if i == 0 else tiles[("qk", g)][:, i - 1, :]
             rows = slice(g * GROUP, (g + 1) * GROUP)
-            bo = psO.tile([P, 512], F32, tag="bo", name="bo")
+            bo = psT.tile([P, 512], F32, tag="bank", name="bo")
             for t in range(TG):
                 nc.tensor.transpose(
                     out=bo[:, t * P : (t + 1) * P], in_=src[:, t * P : (t + 1) * P], identity=ident[:]

@@ -25,8 +25,8 @@ PASSES = D // 512
 FLOPS = 2 * ROWS * D * F
 
 XHAT_ENGINE = ("g", "g", "g", "s")
-LOAD_AHEAD = 4
-STAT_AHEAD = 3
+LOAD_AHEAD = 5
+STAT_AHEAD = 4
 XHAT_AHEAD = 2
 
 
@@ -44,8 +44,8 @@ def tile_gaublock_pb_t_kernel(
 
     with ExitStack() as ctx:
         const = ctx.enter_context(tc.tile_pool(name="const", bufs=1))
-        xpool = ctx.enter_context(tc.tile_pool(name="xpool", bufs=LOAD_AHEAD))
-        small = ctx.enter_context(tc.tile_pool(name="small", bufs=4))
+        xpool = ctx.enter_context(tc.tile_pool(name="xpool", bufs=LOAD_AHEAD + 1))
+        small = ctx.enter_context(tc.tile_pool(name="small", bufs=6))
         xhpool = ctx.enter_context(tc.tile_pool(name="xhpool", bufs=2))
         work = ctx.enter_context(tc.tile_pool(name="work", bufs=2))
         outp = ctx.enter_context(tc.tile_pool(name="outp", bufs=3))
@@ -105,14 +105,21 @@ def tile_gaublock_pb_t_kernel(
                 in_=wgrp[:].rearrange("p c f t -> p (c f t)"),
             )
 
-        def stats(g):
+        def stats_tile(g, t):
+            if t == 0:
+                tiles[("st", g)] = small.tile([P, TG, 2, 6], F32, name="st")
+                tiles[("mv", g)] = small.tile([P, TG, 2], F32, name="mv")
             xt = tiles[("x", g)]
-            st = small.tile([P, TG, 2, 6], F32, name="st")
-            mv = small.tile([P, TG, 2], F32, name="mv")
-            for t in range(TG):
-                for h in range(2):
-                    nc.vector.bn_stats(out=st[:, t, h, :], in_=xt[:, t, h * 512 : (h + 1) * 512])
-                nc.vector.bn_aggr(out=mv[:, t, :], in_=st[:, t, :, :].rearrange("p h s -> p (h s)"))
+            for h in range(2):
+                nc.vector.bn_stats(out=tiles[("st", g)][:, t, h, :], in_=xt[:, t, h * 512 : (h + 1) * 512])
+
+        def aggregate(g, t):
+            nc.vector.bn_aggr(
+                out=tiles[("mv", g)][:, t, :], in_=tiles[("st", g)][:, t, :, :].rearrange("p h s -> p (h s)")
+            )
+
+        def row_scalars(g):
+            mv = tiles[("mv", g)]
             negmu = small.tile([P, TG], F32, name="negmu")
             ve = small.tile([P, TG], F32, name="ve")
             rstd = small.tile([P, TG], F32, name="rstd")
@@ -122,13 +129,14 @@ def tile_gaublock_pb_t_kernel(
             tiles[("negmu", g)] = negmu
             tiles[("rstd", g)] = rstd
 
-        def xhat_prepare(g):
+        def scalar_bias(g):
             nmr = small.tile([P, TG], F32, name="nmr")
             nc.vector.tensor_tensor(out=nmr[:], in0=tiles[("negmu", g)][:], in1=tiles[("rstd", g)][:], op=ALU.mult)
             tiles[("nmr", g)] = nmr
-            tiles[("xh", g)] = xhpool.tile([P, TG, D], F32, name="xh")
 
         def xhat(g, t):
+            if ("xh", g) not in tiles:
+                tiles[("xh", g)] = xhpool.tile([P, TG, D], F32, name="xh")
             xt = tiles[("x", g)]
             xh = tiles[("xh", g)]
             e = XHAT_ENGINE[t]
@@ -159,18 +167,22 @@ def tile_gaublock_pb_t_kernel(
                 bias=prm[:, 8 + j : 9 + j], scale=prm[:, j : j + 1],
             )
 
-        def quantise(g):
+        def regroup(g):
             planes = tiles[("planes", g)]
             grouped = work.tile([P, PASSES, GROUP, 4], BF16, align_bytes=64, name="grouped")
+            tiles[("grouped", g)] = grouped
             for c in range(PASSES):
                 nc.vector.tensor_copy(
                     out=grouped[:, c].rearrange("p (w i) t -> p w t i", i=4),
                     in_=planes[:, c].rearrange("p t (w i) -> p w t i", i=4),
                 )
+
+        def quantise(g):
             codes = work.tile([P, PASSES * GROUP], U32, align_bytes=64, name="codes")
             sc = work.tile([P, PASSES * GROUP], U8, align_bytes=64, name="sc")
             nc.vector.quantize_mx(
-                out=codes[:].bitcast(FP8X4), scales=sc[:], in_=grouped[:].rearrange("p c n t -> p (c n t)")
+                out=codes[:].bitcast(FP8X4), scales=sc[:],
+                in_=tiles[("grouped", g)][:].rearrange("p c n t -> p (c n t)"),
             )
             tiles[("codes", g)] = codes
             tiles[("sc", g)] = sc
@@ -240,35 +252,52 @@ def tile_gaublock_pb_t_kernel(
         def live(g):
             return 0 <= g < NG
 
+        on_gpsimd = [t for t in range(TG) if XHAT_ENGINE[t] != "s"]
+        on_scalar = [t for t in range(TG) if XHAT_ENGINE[t] == "s"]
         for i in range(-STAT_AHEAD, NG + 1):
             if i >= 0 and live(i + LOAD_AHEAD):
                 load(i + LOAD_AHEAD)
             gx = i + XHAT_AHEAD
             gs = i + STAT_AHEAD
             if live(i):
-                quantise(i)
+                regroup(i)
             if live(i - 1):
                 scale_offset(i - 1)
+            if live(i):
+                quantise(i)
+            if live(gs - 1):
+                aggregate(gs - 1, 3)
             if live(gx):
-                xhat_prepare(gx)
-                for t in range(TG):
-                    if XHAT_ENGINE[t] != "s":
-                        xhat(gx, t)
+                xhat(gx, on_gpsimd[0])
+            if live(gs):
+                stats_tile(gs, 0)
+            if live(gs - 1):
+                row_scalars(gs - 1)
+            if live(gx):
+                for t in on_gpsimd[1:]:
+                    xhat(gx, t)
+            if live(gs):
+                stats_tile(gs, 1)
+                aggregate(gs, 0)
+                stats_tile(gs, 2)
+                aggregate(gs, 1)
+            if live(gs - 1):
+                scalar_bias(gs - 1)
+            if live(gs):
+                stats_tile(gs, 3)
+                aggregate(gs, 2)
+            if gs == 0:
+                prepare_params()
+            if gs == 1:
+                prepare_w()
             if live(i + 1):
                 for j in range(8):
                     turn(i + 1, j)
             if live(gx):
-                for t in range(TG):
-                    if XHAT_ENGINE[t] == "s":
-                        xhat(gx, t)
+                for t in on_scalar:
+                    xhat(gx, t)
             if live(i):
                 multiply(i)
             if live(i - 1):
                 for k in range(3):
                     emit_out(i - 1, k)
-            if live(gs):
-                stats(gs)
-            if gs == 0:
-                prepare_params()
-            if gs == 1:
-                prepare_w()

@@ -153,15 +153,19 @@ def tile_gaublock_pb_t_kernel(
                     op0=ALU.add, op1=ALU.mult,
                 )
 
+        def flip(out, in_, as_matmul):
+            if as_matmul:
+                nc.tensor.matmul(out=out, lhsT=in_, rhs=ident[:], start=True, stop=True)
+            else:
+                nc.tensor.transpose(out=out, in_=in_, identity=ident[:])
+
         def turn(g, j):
             if j == 0:
                 tiles[("planes", g)] = work.tile([P, PASSES, 4, GROUP], BF16, name="planes")
             xh = tiles[("xh", g)]
             bank = psT.tile([P, GROUP], F32, tag="bank", name="bank")
             for t in range(TG):
-                nc.tensor.transpose(
-                    out=bank[:, t * P : (t + 1) * P], in_=xh[:, t, j * P : (j + 1) * P], identity=ident[:]
-                )
+                flip(bank[:, t * P : (t + 1) * P], xh[:, t, j * P : (j + 1) * P], t == 0 and j % 2 == 0)
             nc.scalar.activation(
                 out=tiles[("planes", g)][:, j // 4, j % 4, :], in_=bank[:], func=ACT.Identity,
                 bias=prm[:, 8 + j : 9 + j], scale=prm[:, j : j + 1],
@@ -228,9 +232,7 @@ def tile_gaublock_pb_t_kernel(
             rows = slice(g * GROUP, (g + 1) * GROUP)
             bo = psT.tile([P, 512], F32, tag="bank", name="bo")
             for t in range(TG):
-                nc.tensor.transpose(
-                    out=bo[:, t * P : (t + 1) * P], in_=src[:, t * P : (t + 1) * P], identity=ident[:]
-                )
+                flip(bo[:, t * P : (t + 1) * P], src[:, t * P : (t + 1) * P], t == 0 and i != 1)
             if i == 0:
                 st_uv = outp.tile([P, 2, TG, E], F32, name="st_uv")
                 nc.scalar.copy(

@@ -24,7 +24,8 @@ NG = ROWS // GROUP
 PASSES = D // 512
 FLOPS = 2 * ROWS * D * F
 
-XHAT_ENGINE = ("g", "g", "g", "s")
+XHAT_ENGINE = ("g", "g", "v", "s")
+LAST_ON_VECTOR = 2
 LOAD_AHEAD = 5
 STAT_AHEAD = 4
 XHAT_AHEAD = 2
@@ -122,11 +123,14 @@ def tile_gaublock_pb_t_kernel(
             mv = tiles[("mv", g)]
             negmu = small.tile([P, TG], F32, name="negmu")
             ve = small.tile([P, TG], F32, name="ve")
-            rstd = small.tile([P, TG], F32, name="rstd")
             nc.vector.tensor_scalar(out=negmu[:], in0=mv[:, :, 0], scalar1=-1.0, scalar2=None, op0=ALU.mult)
             nc.vector.tensor_scalar(out=ve[:], in0=mv[:, :, 1], scalar1=LN_EPS, scalar2=None, op0=ALU.add)
-            nc.gpsimd.tensor_tensor(out=rstd[:], in0=ve[:], in1=mhalf[:], op=ALU.pow)
             tiles[("negmu", g)] = negmu
+            tiles[("ve", g)] = ve
+
+        def inverse_std(g):
+            rstd = small.tile([P, TG], F32, name="rstd")
+            nc.gpsimd.tensor_tensor(out=rstd[:], in0=tiles[("ve", g)][:], in1=mhalf[:], op=ALU.pow)
             tiles[("rstd", g)] = rstd
 
         def scalar_bias(g):
@@ -134,12 +138,15 @@ def tile_gaublock_pb_t_kernel(
             nc.vector.tensor_tensor(out=nmr[:], in0=tiles[("negmu", g)][:], in1=tiles[("rstd", g)][:], op=ALU.mult)
             tiles[("nmr", g)] = nmr
 
+        def engine_of(g, t):
+            return "v" if g >= NG - LAST_ON_VECTOR else XHAT_ENGINE[t]
+
         def xhat(g, t):
             if ("xh", g) not in tiles:
                 tiles[("xh", g)] = xhpool.tile([P, TG, D], F32, name="xh")
             xt = tiles[("x", g)]
             xh = tiles[("xh", g)]
-            e = XHAT_ENGINE[t]
+            e = engine_of(g, t)
             if e == "s":
                 nc.scalar.activation(
                     out=xh[:, t, :], in_=xt[:, t, :], func=ACT.Identity,
@@ -153,33 +160,27 @@ def tile_gaublock_pb_t_kernel(
                     op0=ALU.add, op1=ALU.mult,
                 )
 
-        def flip(out, in_, as_matmul):
-            if as_matmul:
-                nc.tensor.matmul(out=out, lhsT=in_, rhs=ident[:], start=True, stop=True)
-            else:
-                nc.tensor.transpose(out=out, in_=in_, identity=ident[:])
-
         def turn(g, j):
             if j == 0:
                 tiles[("planes", g)] = work.tile([P, PASSES, 4, GROUP], BF16, name="planes")
             xh = tiles[("xh", g)]
             bank = psT.tile([P, GROUP], F32, tag="bank", name="bank")
             for t in range(TG):
-                flip(bank[:, t * P : (t + 1) * P], xh[:, t, j * P : (j + 1) * P], t == 0 and j % 2 == 0)
+                nc.tensor.transpose(
+                    out=bank[:, t * P : (t + 1) * P], in_=xh[:, t, j * P : (j + 1) * P], identity=ident[:]
+                )
             nc.scalar.activation(
                 out=tiles[("planes", g)][:, j // 4, j % 4, :], in_=bank[:], func=ACT.Identity,
                 bias=prm[:, 8 + j : 9 + j], scale=prm[:, j : j + 1],
             )
 
-        def regroup(g):
-            planes = tiles[("planes", g)]
-            grouped = work.tile([P, PASSES, GROUP, 4], BF16, align_bytes=64, name="grouped")
-            tiles[("grouped", g)] = grouped
-            for c in range(PASSES):
-                nc.vector.tensor_copy(
-                    out=grouped[:, c].rearrange("p (w i) t -> p w t i", i=4),
-                    in_=planes[:, c].rearrange("p t (w i) -> p w t i", i=4),
-                )
+        def regroup(g, c):
+            if c == 0:
+                tiles[("grouped", g)] = work.tile([P, PASSES, GROUP, 4], BF16, align_bytes=64, name="grouped")
+            nc.vector.tensor_copy(
+                out=tiles[("grouped", g)][:, c].rearrange("p (w i) t -> p w t i", i=4),
+                in_=tiles[("planes", g)][:, c].rearrange("p t (w i) -> p w t i", i=4),
+            )
 
         def quantise(g):
             codes = work.tile([P, PASSES * GROUP], U32, align_bytes=64, name="codes")
@@ -232,7 +233,9 @@ def tile_gaublock_pb_t_kernel(
             rows = slice(g * GROUP, (g + 1) * GROUP)
             bo = psT.tile([P, 512], F32, tag="bank", name="bo")
             for t in range(TG):
-                flip(bo[:, t * P : (t + 1) * P], src[:, t * P : (t + 1) * P], t == 0 and i != 1)
+                nc.tensor.transpose(
+                    out=bo[:, t * P : (t + 1) * P], in_=src[:, t * P : (t + 1) * P], identity=ident[:]
+                )
             if i == 0:
                 st_uv = outp.tile([P, 2, TG, E], F32, name="st_uv")
                 nc.scalar.copy(
@@ -254,38 +257,41 @@ def tile_gaublock_pb_t_kernel(
         def live(g):
             return 0 <= g < NG
 
-        on_gpsimd = [t for t in range(TG) if XHAT_ENGINE[t] != "s"]
-        on_scalar = [t for t in range(TG) if XHAT_ENGINE[t] == "s"]
         for i in range(-STAT_AHEAD, NG + 1):
             if i >= 0 and live(i + LOAD_AHEAD):
                 load(i + LOAD_AHEAD)
             gx = i + XHAT_AHEAD
             gs = i + STAT_AHEAD
             if live(i):
-                regroup(i)
-            if live(i - 1):
-                scale_offset(i - 1)
-            if live(i):
-                quantise(i)
+                regroup(i, 0)
             if live(gs - 1):
                 aggregate(gs - 1, 3)
-            if live(gx):
-                xhat(gx, on_gpsimd[0])
-            if live(gs):
-                stats_tile(gs, 0)
+            if live(i):
+                regroup(i, 1)
+            if live(gx) and engine_of(gx, TG - 1) == "s":
+                scalar_bias(gx)
+            if live(i - 1):
+                scale_offset(i - 1)
             if live(gs - 1):
                 row_scalars(gs - 1)
             if live(gx):
-                for t in on_gpsimd[1:]:
-                    xhat(gx, t)
+                for t in range(TG):
+                    if engine_of(gx, t) == "v":
+                        xhat(gx, t)
+            if live(i):
+                quantise(i)
+            if live(gs - 1):
+                inverse_std(gs - 1)
+            if live(gx):
+                for t in range(TG):
+                    if engine_of(gx, t) == "g":
+                        xhat(gx, t)
             if live(gs):
+                stats_tile(gs, 0)
                 stats_tile(gs, 1)
                 aggregate(gs, 0)
                 stats_tile(gs, 2)
                 aggregate(gs, 1)
-            if live(gs - 1):
-                scalar_bias(gs - 1)
-            if live(gs):
                 stats_tile(gs, 3)
                 aggregate(gs, 2)
             if gs == 0:
@@ -296,8 +302,9 @@ def tile_gaublock_pb_t_kernel(
                 for j in range(8):
                     turn(i + 1, j)
             if live(gx):
-                for t in on_scalar:
-                    xhat(gx, t)
+                for t in range(TG):
+                    if engine_of(gx, t) == "s":
+                        xhat(gx, t)
             if live(i):
                 multiply(i)
             if live(i - 1):

@@ -12,30 +12,47 @@ ACT = mybir.ActivationFunctionType
 ALU = mybir.AluOpType
 
 P = 128
-ROWS = 8192
+ROWS = 8 * 1024
 D = 1024
 F = 256
 E = 64
 S = 128
 LN_EPS = 1e-5
-TG = 4
-GROUP = TG * P
-NG = ROWS // GROUP
-PASSES = D // 512
+PACK = 4
+K_PASS = P * PACK
+PASSES = D // K_PASS
+K_BLOCKS = D // P
+TILES = 4
+GROUP = TILES * P
+GROUPS = ROWS // GROUP
+BN_MAX = 512
 FLOPS = 2 * ROWS * D * F
 
-XHAT_ENGINE = ("g", "g", "v", "s")
-LAST_ON_VECTOR = 2
 LOAD_AHEAD = 5
 STAT_AHEAD = 4
 XHAT_AHEAD = 2
+
+XHAT_SHARES = (
+    ("gpsimd", 0, 0, D),
+    ("gpsimd", 1, 0, D),
+    ("vector", 2, 0, D // 2),
+    ("scalar", 2, D // 2, D),
+    ("scalar", 3, 0, D),
+)
+XHAT_SHARES_AT_END = (("vector", 0, 0, D), ("vector", 1, 0, D), ("vector", 2, 0, D), ("vector", 3, 0, D))
+
+COL_G = 0
+COL_B = COL_G + K_BLOCKS
+COL_BIAS = COL_B + K_BLOCKS
+COL_GAMMA_BETA = COL_BIAS + F // P
+PARAM_COLS = 32
 
 
 def tile_gaublock_pb_t_kernel(
     tc, x, ln_g, ln_b, W_in, b_in, gamma_q, beta_q, gamma_k, beta_k, out_0, out_1, out_2, out_3
 ):
     nc = tc.nc
-    xf = x.flatten_outer_dims()
+    x_rows = x.flatten_outer_dims()
     outs = (
         out_0.flatten_outer_dims(),
         out_1.flatten_outer_dims(),
@@ -45,23 +62,28 @@ def tile_gaublock_pb_t_kernel(
 
     with ExitStack() as ctx:
         const = ctx.enter_context(tc.tile_pool(name="const", bufs=1))
-        xpool = ctx.enter_context(tc.tile_pool(name="xpool", bufs=LOAD_AHEAD + 1))
-        small = ctx.enter_context(tc.tile_pool(name="small", bufs=6))
-        xhpool = ctx.enter_context(tc.tile_pool(name="xhpool", bufs=2))
+        x_pool = ctx.enter_context(tc.tile_pool(name="x_pool", bufs=LOAD_AHEAD + 1))
+        row_pool = ctx.enter_context(tc.tile_pool(name="row_pool", bufs=STAT_AHEAD + 2))
         work = ctx.enter_context(tc.tile_pool(name="work", bufs=2))
-        outp = ctx.enter_context(tc.tile_pool(name="outp", bufs=3))
-        psT = ctx.enter_context(tc.psum_pool(name="psT", bufs=6))
-        psM = ctx.enter_context(tc.psum_pool(name="psM", bufs=2))
+        store_pool = ctx.enter_context(tc.tile_pool(name="store_pool", bufs=3))
+        turn_banks = ctx.enter_context(tc.psum_pool(name="turn_banks", bufs=6))
+        mx_banks = ctx.enter_context(tc.psum_pool(name="mx_banks", bufs=2))
         ctx.enter_context(tc.manual_schedule())
 
         tiles = {}
 
+        def live(g):
+            return 0 <= g < GROUPS
+
+        def shares(g):
+            return XHAT_SHARES_AT_END if g >= GROUPS - STAT_AHEAD + XHAT_AHEAD else XHAT_SHARES
+
         def load(g):
-            xt = xpool.tile([P, TG, D], BF16, name="xt")
+            xt = x_pool.tile([P, TILES, D], BF16, name="xt")
             tiles[("x", g)] = xt
-            src = xf[g * GROUP : (g + 1) * GROUP, :].rearrange("(p t) k -> p t k", t=TG)
+            src = x_rows[g * GROUP : (g + 1) * GROUP, :].rearrange("(p t) k -> p t k", t=TILES)
             if g == 0:
-                for t in range(TG):
+                for t in range(TILES):
                     nc.sync.dma_start(out=xt[:, t, :], in_=src[:, t, :])
             else:
                 nc.sync.dma_start(out=xt[:], in_=src)
@@ -69,242 +91,237 @@ def tile_gaublock_pb_t_kernel(
         load(0)
         ident = const.tile([P, P], F32)
         make_identity(nc, ident[:])
-        mhalf = const.tile([P, TG], F32)
-        nc.vector.memset(mhalf[:], -0.5)
-        prm_bf = const.tile([P, P], BF16)
-        nc.vector.memset(prm_bf[:], 0.0)
-        nc.scalar.dma_start(out=prm_bf[0:8, :], in_=ln_g.rearrange("(j p) -> j p", p=P))
-        nc.scalar.dma_start(out=prm_bf[8:16, :], in_=ln_b.rearrange("(j p) -> j p", p=P))
-        nc.scalar.dma_start(out=prm_bf[16:18, :], in_=b_in.rearrange("(j p) -> j p", p=P))
-        nc.scalar.dma_start(out=prm_bf[18:19, :], in_=gamma_q.rearrange("(j p) -> j p", p=P))
-        nc.scalar.dma_start(out=prm_bf[19:20, :], in_=beta_q.rearrange("(j p) -> j p", p=P))
-        nc.scalar.dma_start(out=prm_bf[20:21, :], in_=gamma_k.rearrange("(j p) -> j p", p=P))
-        nc.scalar.dma_start(out=prm_bf[21:22, :], in_=beta_k.rearrange("(j p) -> j p", p=P))
+        minus_half = const.tile([P, TILES], F32)
+        nc.vector.memset(minus_half[:], -0.5)
+        param_rows = const.tile([P, P], BF16)
+        nc.vector.memset(param_rows[:], 0.0)
+        row = 0
+        for vec in (ln_g, ln_b, b_in, gamma_q, beta_q, gamma_k, beta_k):
+            n = vec.shape[0] // P
+            nc.scalar.dma_start(out=param_rows[row : row + n, :], in_=vec.rearrange("(j p) -> j p", p=P))
+            row += n
         load(1)
-        wraw = const.tile([P, PASSES * 4, F], BF16)
-        nc.sync.dma_start(out=wraw[:], in_=W_in.rearrange("(j p) f -> p j f", p=P))
+        w_raw = const.tile([P, K_BLOCKS, F], BF16)
+        nc.sync.dma_start(out=w_raw[:], in_=W_in.rearrange("(j p) f -> p j f", p=P))
         for g in range(2, LOAD_AHEAD):
             load(g)
 
-        prm = const.tile([P, 32], F32)
-        wcodes = const.tile([P, PASSES * F], U32, align_bytes=64)
-        wsc = const.tile([P, PASSES * F], U8, align_bytes=64)
+        params = const.tile([P, PARAM_COLS], F32)
+        w_codes = const.tile([P, PASSES * F], U32, align_bytes=64)
+        w_scales = const.tile([P, PASSES * F], U8, align_bytes=64)
+
+        def param(col):
+            return params[:, col : col + 1]
 
         def prepare_params():
-            prm_f = const.tile([P, P], F32)
-            nc.vector.tensor_copy(out=prm_f[:], in_=prm_bf[:])
-            prm_ps = psT.tile([P, 512], F32, tag="bank", name="prm_ps")
-            nc.tensor.transpose(out=prm_ps[:, 0:P], in_=prm_f[:], identity=ident[:])
-            nc.vector.tensor_copy(out=prm[:], in_=prm_ps[:, 0:32])
+            param_f32 = const.tile([P, P], F32)
+            nc.vector.tensor_copy(out=param_f32[:], in_=param_rows[:])
+            bank = turn_banks.tile([P, GROUP], F32, tag="bank", name="param_bank")
+            nc.tensor.transpose(out=bank[:, 0:P], in_=param_f32[:], identity=ident[:])
+            nc.vector.tensor_copy(out=params[:], in_=bank[:, 0:PARAM_COLS])
 
         def prepare_w():
-            wgrp = const.tile([P, PASSES, F, 4], BF16, align_bytes=64)
-            nc.vector.tensor_copy(out=wgrp[:], in_=wraw[:].rearrange("p (c t) f -> p c f t", t=4))
+            w_words = const.tile([P, PASSES, F, PACK], BF16, align_bytes=64)
+            nc.vector.tensor_copy(out=w_words[:], in_=w_raw[:].rearrange("p (c t) f -> p c f t", t=PACK))
             nc.vector.quantize_mx(
-                out=wcodes[:].bitcast(FP8X4),
-                scales=wsc[:],
-                in_=wgrp[:].rearrange("p c f t -> p (c f t)"),
+                out=w_codes[:].bitcast(FP8X4),
+                scales=w_scales[:],
+                in_=w_words[:].rearrange("p c f t -> p (c f t)"),
             )
 
         def stats_tile(g, t):
             if t == 0:
-                tiles[("st", g)] = small.tile([P, TG, 2, 6], F32, name="st")
-                tiles[("mv", g)] = small.tile([P, TG, 2], F32, name="mv")
-            xt = tiles[("x", g)]
-            for h in range(2):
-                nc.vector.bn_stats(out=tiles[("st", g)][:, t, h, :], in_=xt[:, t, h * 512 : (h + 1) * 512])
+                tiles[("stats", g)] = row_pool.tile([P, TILES, D // BN_MAX, 6], F32, name="stats")
+                tiles[("mean_var", g)] = row_pool.tile([P, TILES, 2], F32, name="mean_var")
+            for h in range(D // BN_MAX):
+                nc.vector.bn_stats(
+                    out=tiles[("stats", g)][:, t, h, :], in_=tiles[("x", g)][:, t, h * BN_MAX : (h + 1) * BN_MAX]
+                )
 
         def aggregate(g, t):
             nc.vector.bn_aggr(
-                out=tiles[("mv", g)][:, t, :], in_=tiles[("st", g)][:, t, :, :].rearrange("p h s -> p (h s)")
+                out=tiles[("mean_var", g)][:, t, :],
+                in_=tiles[("stats", g)][:, t, :, :].rearrange("p h s -> p (h s)"),
             )
 
         def row_scalars(g):
-            mv = tiles[("mv", g)]
-            negmu = small.tile([P, TG], F32, name="negmu")
-            ve = small.tile([P, TG], F32, name="ve")
-            nc.vector.tensor_scalar(out=negmu[:], in0=mv[:, :, 0], scalar1=-1.0, scalar2=None, op0=ALU.mult)
-            nc.vector.tensor_scalar(out=ve[:], in0=mv[:, :, 1], scalar1=LN_EPS, scalar2=None, op0=ALU.add)
-            tiles[("negmu", g)] = negmu
-            tiles[("ve", g)] = ve
+            mean_var = tiles[("mean_var", g)]
+            neg_mean = row_pool.tile([P, TILES], F32, name="neg_mean")
+            var_eps = row_pool.tile([P, TILES], F32, name="var_eps")
+            nc.vector.tensor_scalar(out=neg_mean[:], in0=mean_var[:, :, 0], scalar1=-1.0, scalar2=None, op0=ALU.mult)
+            nc.vector.tensor_scalar(out=var_eps[:], in0=mean_var[:, :, 1], scalar1=LN_EPS, scalar2=None, op0=ALU.add)
+            tiles[("neg_mean", g)] = neg_mean
+            tiles[("var_eps", g)] = var_eps
 
         def inverse_std(g):
-            rstd = small.tile([P, TG], F32, name="rstd")
-            nc.gpsimd.tensor_tensor(out=rstd[:], in0=tiles[("ve", g)][:], in1=mhalf[:], op=ALU.pow)
+            rstd = row_pool.tile([P, TILES], F32, name="rstd")
+            nc.gpsimd.tensor_tensor(out=rstd[:], in0=tiles[("var_eps", g)][:], in1=minus_half[:], op=ALU.pow)
             tiles[("rstd", g)] = rstd
 
         def scalar_bias(g):
-            nmr = small.tile([P, TG], F32, name="nmr")
-            nc.vector.tensor_tensor(out=nmr[:], in0=tiles[("negmu", g)][:], in1=tiles[("rstd", g)][:], op=ALU.mult)
-            tiles[("nmr", g)] = nmr
+            bias = row_pool.tile([P, TILES], F32, name="bias")
+            nc.vector.tensor_tensor(
+                out=bias[:], in0=tiles[("neg_mean", g)][:], in1=tiles[("rstd", g)][:], op=ALU.mult
+            )
+            tiles[("bias", g)] = bias
 
-        def engine_of(g, t):
-            return "v" if g >= NG - LAST_ON_VECTOR else XHAT_ENGINE[t]
-
-        def xhat(g, t):
-            if ("xh", g) not in tiles:
-                tiles[("xh", g)] = xhpool.tile([P, TG, D], F32, name="xh")
-            xt = tiles[("x", g)]
-            xh = tiles[("xh", g)]
-            e = engine_of(g, t)
-            if e == "s":
-                nc.scalar.activation(
-                    out=xh[:, t, :], in_=xt[:, t, :], func=ACT.Identity,
-                    bias=tiles[("nmr", g)][:, t : t + 1], scale=tiles[("rstd", g)][:, t : t + 1],
-                )
-            else:
-                eng = nc.gpsimd if e == "g" else nc.vector
-                eng.tensor_scalar(
-                    out=xh[:, t, :], in0=xt[:, t, :],
-                    scalar1=tiles[("negmu", g)][:, t : t + 1], scalar2=tiles[("rstd", g)][:, t : t + 1],
-                    op0=ALU.add, op1=ALU.mult,
-                )
+        def xhat(g, engine):
+            if ("xhat", g) not in tiles:
+                tiles[("xhat", g)] = work.tile([P, TILES, D], F32, name="xhat")
+            for t, lo, hi in [share[1:] for share in shares(g) if share[0] == engine]:
+                dst = tiles[("xhat", g)][:, t, lo:hi]
+                src = tiles[("x", g)][:, t, lo:hi]
+                rstd = tiles[("rstd", g)][:, t : t + 1]
+                if engine == "scalar":
+                    nc.scalar.activation(
+                        out=dst, in_=src, func=ACT.Identity, bias=tiles[("bias", g)][:, t : t + 1], scale=rstd
+                    )
+                else:
+                    eng = nc.gpsimd if engine == "gpsimd" else nc.vector
+                    eng.tensor_scalar(
+                        out=dst, in0=src, scalar1=tiles[("neg_mean", g)][:, t : t + 1], scalar2=rstd,
+                        op0=ALU.add, op1=ALU.mult,
+                    )
 
         def turn(g, j):
             if j == 0:
-                tiles[("planes", g)] = work.tile([P, PASSES, 4, GROUP], BF16, name="planes")
-            xh = tiles[("xh", g)]
-            bank = psT.tile([P, GROUP], F32, tag="bank", name="bank")
-            for t in range(TG):
+                tiles[("planes", g)] = work.tile([P, PASSES, PACK, GROUP], BF16, name="planes")
+            bank = turn_banks.tile([P, GROUP], F32, tag="bank", name="bank")
+            for t in range(TILES):
                 nc.tensor.transpose(
-                    out=bank[:, t * P : (t + 1) * P], in_=xh[:, t, j * P : (j + 1) * P], identity=ident[:]
+                    out=bank[:, t * P : (t + 1) * P],
+                    in_=tiles[("xhat", g)][:, t, j * P : (j + 1) * P],
+                    identity=ident[:],
                 )
             nc.scalar.activation(
-                out=tiles[("planes", g)][:, j // 4, j % 4, :], in_=bank[:], func=ACT.Identity,
-                bias=prm[:, 8 + j : 9 + j], scale=prm[:, j : j + 1],
+                out=tiles[("planes", g)][:, j // PACK, j % PACK, :], in_=bank[:], func=ACT.Identity,
+                bias=param(COL_B + j), scale=param(COL_G + j),
             )
 
         def regroup(g, c):
             if c == 0:
-                tiles[("grouped", g)] = work.tile([P, PASSES, GROUP, 4], BF16, align_bytes=64, name="grouped")
+                tiles[("words", g)] = work.tile([P, PASSES, GROUP, PACK], BF16, align_bytes=64, name="words")
             nc.vector.tensor_copy(
-                out=tiles[("grouped", g)][:, c].rearrange("p (w i) t -> p w t i", i=4),
+                out=tiles[("words", g)][:, c].rearrange("p (w i) t -> p w t i", i=4),
                 in_=tiles[("planes", g)][:, c].rearrange("p t (w i) -> p w t i", i=4),
             )
 
         def quantise(g):
             codes = work.tile([P, PASSES * GROUP], U32, align_bytes=64, name="codes")
-            sc = work.tile([P, PASSES * GROUP], U8, align_bytes=64, name="sc")
+            scales = work.tile([P, PASSES * GROUP], U8, align_bytes=64, name="scales")
             nc.vector.quantize_mx(
-                out=codes[:].bitcast(FP8X4), scales=sc[:],
-                in_=tiles[("grouped", g)][:].rearrange("p c n t -> p (c n t)"),
+                out=codes[:].bitcast(FP8X4), scales=scales[:],
+                in_=tiles[("words", g)][:].rearrange("p c n t -> p (c n t)"),
             )
             tiles[("codes", g)] = codes
-            tiles[("sc", g)] = sc
+            tiles[("scales", g)] = scales
 
         def multiply(g):
             codes = tiles[("codes", g)]
-            sc = tiles[("sc", g)]
-            sil = work.tile([P, 2, GROUP], F32, name="sil")
-            tiles[("sil", g)] = sil
+            scales = tiles[("scales", g)]
+            silu = work.tile([P, F // P, GROUP], F32, name="silu")
+            tiles[("silu", g)] = silu
             accs = []
-            for h in range(2):
-                acc = psM.tile([P, GROUP], F32, name="acc")
+            for h in range(F // P):
+                acc = mx_banks.tile([P, GROUP], F32, name="acc")
                 accs.append(acc)
                 for c in range(PASSES):
                     w0 = c * F + h * P
                     nc.tensor.matmul_mx(
                         out=acc[:],
-                        lhsT=wcodes[:, w0 : w0 + P].bitcast(FP8X4),
-                        lhsT_scale=wsc[:, w0 : w0 + P],
+                        lhsT=w_codes[:, w0 : w0 + P].bitcast(FP8X4),
+                        lhsT_scale=w_scales[:, w0 : w0 + P],
                         rhs=codes[:, c * GROUP : (c + 1) * GROUP].bitcast(FP8X4),
-                        rhs_scale=sc[:, c * GROUP : (c + 1) * GROUP],
+                        rhs_scale=scales[:, c * GROUP : (c + 1) * GROUP],
                         start=(c == 0),
                         stop=(c == PASSES - 1),
                     )
-            for h in range(2):
+            for h in range(F // P):
                 nc.scalar.activation(
-                    out=sil[:, h, :], in_=accs[h][:], func=ACT.Silu, bias=prm[:, 16 + h : 17 + h], scale=1.0
+                    out=silu[:, h, :], in_=accs[h][:], func=ACT.Silu, bias=param(COL_BIAS + h), scale=1.0
                 )
 
         def scale_offset(g):
-            sil = tiles[("sil", g)]
+            z = tiles[("silu", g)][:, 1, :]
             qk = work.tile([P, 2, GROUP], F32, name="qk")
             tiles[("qk", g)] = qk
             for i in range(2):
                 nc.vector.tensor_scalar(
-                    out=qk[:, i, :], in0=sil[:, 1, :],
-                    scalar1=prm[:, 18 + 2 * i : 19 + 2 * i], scalar2=prm[:, 19 + 2 * i : 20 + 2 * i],
+                    out=qk[:, i, :], in0=z,
+                    scalar1=param(COL_GAMMA_BETA + 2 * i), scalar2=param(COL_GAMMA_BETA + 2 * i + 1),
                     op0=ALU.mult, op1=ALU.add,
                 )
 
         def emit_out(g, i):
-            src = tiles[("sil", g)][:, 0, :] if i == 0 else tiles[("qk", g)][:, i - 1, :]
+            src = tiles[("silu", g)][:, 0, :] if i == 0 else tiles[("qk", g)][:, i - 1, :]
             rows = slice(g * GROUP, (g + 1) * GROUP)
-            bo = psT.tile([P, 512], F32, tag="bank", name="bo")
-            for t in range(TG):
+            bank = turn_banks.tile([P, GROUP], F32, tag="bank", name="out_bank")
+            for t in range(TILES):
                 nc.tensor.transpose(
-                    out=bo[:, t * P : (t + 1) * P], in_=src[:, t * P : (t + 1) * P], identity=ident[:]
+                    out=bank[:, t * P : (t + 1) * P], in_=src[:, t * P : (t + 1) * P], identity=ident[:]
                 )
             if i == 0:
-                st_uv = outp.tile([P, 2, TG, E], F32, name="st_uv")
+                uv = store_pool.tile([P, 2, TILES, E], F32, name="uv")
                 nc.scalar.copy(
-                    out=st_uv[:].rearrange("p c t f -> p t c f"),
-                    in_=bo[:].rearrange("p (t c f) -> p t c f", t=TG, c=2),
+                    out=uv[:].rearrange("p c t f -> p t c f"),
+                    in_=bank[:].rearrange("p (t c f) -> p t c f", t=TILES, c=2),
                 )
                 for c in range(2):
                     nc.sync.dma_start(
-                        out=outs[c][rows, :].rearrange("(p t) f -> p (t f)", t=TG),
-                        in_=st_uv[:, c].rearrange("p t f -> p (t f)"),
+                        out=outs[c][rows, :].rearrange("(p t) f -> p (t f)", t=TILES),
+                        in_=uv[:, c].rearrange("p t f -> p (t f)"),
                     )
             else:
-                st_o = outp.tile([P, TG * S], F32, name="st_o", bufs=6)
-                nc.scalar.copy(out=st_o[:], in_=bo[:])
+                q_or_k = store_pool.tile([P, TILES * S], F32, name="q_or_k", bufs=6)
+                nc.scalar.copy(out=q_or_k[:], in_=bank[:])
                 nc.sync.dma_start(
-                    out=outs[1 + i][rows, :].rearrange("(p t) f -> p (t f)", t=TG), in_=st_o[:]
+                    out=outs[1 + i][rows, :].rearrange("(p t) f -> p (t f)", t=TILES), in_=q_or_k[:]
                 )
 
-        def live(g):
-            return 0 <= g < NG
-
-        for i in range(-STAT_AHEAD, NG + 1):
+        for i in range(-STAT_AHEAD, GROUPS + 1):
+            g_stat = i + STAT_AHEAD
+            g_xhat = i + XHAT_AHEAD
             if i >= 0 and live(i + LOAD_AHEAD):
                 load(i + LOAD_AHEAD)
-            gx = i + XHAT_AHEAD
-            gs = i + STAT_AHEAD
+
             if live(i):
                 regroup(i, 0)
-            if live(gs - 1):
-                aggregate(gs - 1, 3)
+            if live(g_stat - 1):
+                aggregate(g_stat - 1, TILES - 1)
             if live(i):
                 regroup(i, 1)
-            if live(gx) and engine_of(gx, TG - 1) == "s":
-                scalar_bias(gx)
+            if live(i) and not live(g_stat):
+                quantise(i)
+            if live(g_xhat) and any(share[0] == "scalar" for share in shares(g_xhat)):
+                scalar_bias(g_xhat)
             if live(i - 1):
                 scale_offset(i - 1)
-            if live(gs - 1):
-                row_scalars(gs - 1)
-            if live(gx):
-                for t in range(TG):
-                    if engine_of(gx, t) == "v":
-                        xhat(gx, t)
-            if live(i):
+            if live(g_stat - 1):
+                row_scalars(g_stat - 1)
+            if live(g_xhat):
+                xhat(g_xhat, "vector")
+            if live(i) and live(g_stat):
                 quantise(i)
-            if live(gs - 1):
-                inverse_std(gs - 1)
-            if live(gx):
-                for t in range(TG):
-                    if engine_of(gx, t) == "g":
-                        xhat(gx, t)
-            if live(gs):
-                stats_tile(gs, 0)
-                stats_tile(gs, 1)
-                aggregate(gs, 0)
-                stats_tile(gs, 2)
-                aggregate(gs, 1)
-                stats_tile(gs, 3)
-                aggregate(gs, 2)
-            if gs == 0:
+
+            if live(g_stat - 1):
+                inverse_std(g_stat - 1)
+            if live(g_xhat):
+                xhat(g_xhat, "gpsimd")
+            if live(g_stat):
+                stats_tile(g_stat, 0)
+                for t in range(1, TILES):
+                    stats_tile(g_stat, t)
+                    aggregate(g_stat, t - 1)
+            if g_stat == 0:
                 prepare_params()
-            if gs == 1:
+            if g_stat == 1:
                 prepare_w()
+
             if live(i + 1):
-                for j in range(8):
+                for j in range(K_BLOCKS):
                     turn(i + 1, j)
-            if live(gx):
-                for t in range(TG):
-                    if engine_of(gx, t) == "s":
-                        xhat(gx, t)
+            if live(g_xhat):
+                xhat(g_xhat, "scalar")
             if live(i):
                 multiply(i)
             if live(i - 1):

@@ -28,9 +28,10 @@ GROUPS = ROWS // GROUP
 BN_MAX = 512
 FLOPS = 2 * ROWS * D * F
 
-LOAD_AHEAD = 5
-STAT_AHEAD = 4
+LOAD_AHEAD = 4
+STAT_AHEAD = 3
 XHAT_AHEAD = 2
+assert XHAT_AHEAD == STAT_AHEAD - 1
 
 XHAT_SHARES = (
     ("gpsimd", 0, 0, D),
@@ -39,7 +40,7 @@ XHAT_SHARES = (
     ("scalar", 2, D // 2, D),
     ("scalar", 3, 0, D),
 )
-XHAT_SHARES_AT_END = (("vector", 0, 0, D), ("vector", 1, 0, D), ("vector", 2, 0, D), ("vector", 3, 0, D))
+XHAT_SHARES_OF_LAST = (("vector", 0, 0, D), ("vector", 1, 0, D), ("vector", 2, 0, D), ("vector", 3, 0, D))
 
 COL_G = 0
 COL_B = COL_G + K_BLOCKS
@@ -76,7 +77,7 @@ def tile_gaublock_pb_t_kernel(
             return 0 <= g < GROUPS
 
         def shares(g):
-            return XHAT_SHARES_AT_END if g >= GROUPS - STAT_AHEAD + XHAT_AHEAD else XHAT_SHARES
+            return XHAT_SHARES_OF_LAST if g == GROUPS - 1 else XHAT_SHARES
 
         def load(g):
             xt = x_pool.tile([P, TILES, D], BF16, name="xt")
@@ -160,15 +161,16 @@ def tile_gaublock_pb_t_kernel(
 
         def scalar_bias(g):
             bias = row_pool.tile([P, TILES], F32, name="bias")
-            nc.vector.tensor_tensor(
+            nc.gpsimd.tensor_tensor(
                 out=bias[:], in0=tiles[("neg_mean", g)][:], in1=tiles[("rstd", g)][:], op=ALU.mult
             )
             tiles[("bias", g)] = bias
 
         def xhat(g, engine):
-            if ("xhat", g) not in tiles:
+            mine = [share[1:] for share in shares(g) if share[0] == engine]
+            if mine and ("xhat", g) not in tiles:
                 tiles[("xhat", g)] = work.tile([P, TILES, D], F32, name="xhat")
-            for t, lo, hi in [share[1:] for share in shares(g) if share[0] == engine]:
+            for t, lo, hi in mine:
                 dst = tiles[("xhat", g)][:, t, lo:hi]
                 src = tiles[("x", g)][:, t, lo:hi]
                 rstd = tiles[("rstd", g)][:, t : t + 1]
@@ -284,6 +286,8 @@ def tile_gaublock_pb_t_kernel(
             if i >= 0 and live(i + LOAD_AHEAD):
                 load(i + LOAD_AHEAD)
 
+            if live(g_xhat - 1):
+                xhat(g_xhat - 1, "vector")
             if live(i):
                 regroup(i, 0)
             if live(g_stat - 1):
@@ -292,20 +296,17 @@ def tile_gaublock_pb_t_kernel(
                 regroup(i, 1)
             if live(i) and not live(g_stat):
                 quantise(i)
-            if live(g_xhat) and any(share[0] == "scalar" for share in shares(g_xhat)):
-                scalar_bias(g_xhat)
             if live(i - 1):
                 scale_offset(i - 1)
             if live(g_stat - 1):
                 row_scalars(g_stat - 1)
-            if live(g_xhat):
-                xhat(g_xhat, "vector")
             if live(i) and live(g_stat):
                 quantise(i)
 
-            if live(g_stat - 1):
-                inverse_std(g_stat - 1)
             if live(g_xhat):
+                inverse_std(g_xhat)
+                if any(share[0] == "scalar" for share in shares(g_xhat)):
+                    scalar_bias(g_xhat)
                 xhat(g_xhat, "gpsimd")
             if live(g_stat):
                 stats_tile(g_stat, 0)

from contextlib import ExitStack

import concourse.mybir as mybir
from concourse.masks import make_identity

F32 = mybir.dt.float32
BF16 = mybir.dt.bfloat16
U32 = mybir.dt.uint32
U8 = mybir.dt.uint8
FP8X4 = mybir.dt.float8_e4m3fn_x4
ACT = mybir.ActivationFunctionType
ALU = mybir.AluOpType

P = 128
ROWS = 8 * 1024
D = 1024
F = 256
E = 64
S = 128
LN_EPS = 1e-5
PACK = 4
K_PASS = P * PACK
PASSES = D // K_PASS
K_BLOCKS = D // P
TILES = 4
GROUP = TILES * P
GROUPS = ROWS // GROUP
BN_MAX = 512
FLOPS = 2 * ROWS * D * F

LOAD_AHEAD = 4
STAT_AHEAD = 3
XHAT_AHEAD = 2
assert XHAT_AHEAD == STAT_AHEAD - 1

XHAT_SHARES = (
    ("gpsimd", 0, 0, D),
    ("gpsimd", 1, 0, D),
    ("vector", 2, 0, D // 2),
    ("scalar", 2, D // 2, D),
    ("scalar", 3, 0, D),
)
XHAT_SHARES_OF_LAST = (("vector", 0, 0, D), ("vector", 1, 0, D), ("vector", 2, 0, D), ("vector", 3, 0, D))

COL_G = 0
COL_B = COL_G + K_BLOCKS
COL_BIAS = COL_B + K_BLOCKS
COL_GAMMA_BETA = COL_BIAS + F // P
PARAM_COLS = 32


def tile_gaublock_pb_t_kernel(
    tc, x, ln_g, ln_b, W_in, b_in, gamma_q, beta_q, gamma_k, beta_k, out_0, out_1, out_2, out_3
):
    nc = tc.nc
    x_rows = x.flatten_outer_dims()
    outs = (
        out_0.flatten_outer_dims(),
        out_1.flatten_outer_dims(),
        out_2.flatten_outer_dims(),
        out_3.flatten_outer_dims(),
    )

    with ExitStack() as ctx:
        const = ctx.enter_context(tc.tile_pool(name="const", bufs=1))
        x_pool = ctx.enter_context(tc.tile_pool(name="x_pool", bufs=LOAD_AHEAD + 1))
        row_pool = ctx.enter_context(tc.tile_pool(name="row_pool", bufs=STAT_AHEAD + 2))
        work = ctx.enter_context(tc.tile_pool(name="work", bufs=2))
        store_pool = ctx.enter_context(tc.tile_pool(name="store_pool", bufs=3))
        turn_banks = ctx.enter_context(tc.psum_pool(name="turn_banks", bufs=6))
        mx_banks = ctx.enter_context(tc.psum_pool(name="mx_banks", bufs=2))
        ctx.enter_context(tc.manual_schedule())

        tiles = {}

        def live(g):
            return 0 <= g < GROUPS

        def shares(g):
            return XHAT_SHARES_OF_LAST if g == GROUPS - 1 else XHAT_SHARES

        def load(g):
            xt = x_pool.tile([P, TILES, D], BF16, name="xt")
            tiles[("x", g)] = xt
            src = x_rows[g * GROUP : (g + 1) * GROUP, :].rearrange("(p t) k -> p t k", t=TILES)
            if g == 0:
                for t in range(TILES):
                    nc.sync.dma_start(out=xt[:, t, :], in_=src[:, t, :])
            else:
                nc.sync.dma_start(out=xt[:], in_=src)

        load(0)
        ident = const.tile([P, P], F32)
        make_identity(nc, ident[:])
        minus_half = const.tile([P, TILES], F32)
        nc.vector.memset(minus_half[:], -0.5)
        param_rows = const.tile([P, P], BF16)
        nc.vector.memset(param_rows[:], 0.0)
        row = 0
        for vec in (ln_g, ln_b, b_in, gamma_q, beta_q, gamma_k, beta_k):
            n = vec.shape[0] // P
            nc.scalar.dma_start(out=param_rows[row : row + n, :], in_=vec.rearrange("(j p) -> j p", p=P))
            row += n
        load(1)
        w_raw = const.tile([P, K_BLOCKS, F], BF16)
        nc.sync.dma_start(out=w_raw[:], in_=W_in.rearrange("(j p) f -> p j f", p=P))
        for g in range(2, LOAD_AHEAD):
            load(g)

        params = const.tile([P, PARAM_COLS], F32)
        w_codes = const.tile([P, PASSES * F], U32, align_bytes=64)
        w_scales = const.tile([P, PASSES * F], U8, align_bytes=64)

        def param(col):
            return params[:, col : col + 1]

        def prepare_params():
            param_f32 = const.tile([P, P], F32)
            nc.vector.tensor_copy(out=param_f32[:], in_=param_rows[:])
            bank = turn_banks.tile([P, GROUP], F32, tag="bank", name="param_bank")
            nc.tensor.transpose(out=bank[:, 0:P], in_=param_f32[:], identity=ident[:])
            nc.vector.tensor_copy(out=params[:], in_=bank[:, 0:PARAM_COLS])

        def prepare_w():
            w_words = const.tile([P, PASSES, F, PACK], BF16, align_bytes=64)
            nc.vector.tensor_copy(out=w_words[:], in_=w_raw[:].rearrange("p (c t) f -> p c f t", t=PACK))
            nc.vector.quantize_mx(
                out=w_codes[:].bitcast(FP8X4),
                scales=w_scales[:],
                in_=w_words[:].rearrange("p c f t -> p (c f t)"),
            )

        def stats_tile(g, t):
            if t == 0:
                tiles[("stats", g)] = row_pool.tile([P, TILES, D // BN_MAX, 6], F32, name="stats")
                tiles[("mean_var", g)] = row_pool.tile([P, TILES, 2], F32, name="mean_var")
            for h in range(D // BN_MAX):
                nc.vector.bn_stats(
                    out=tiles[("stats", g)][:, t, h, :], in_=tiles[("x", g)][:, t, h * BN_MAX : (h + 1) * BN_MAX]
                )

        def aggregate(g, t):
            nc.vector.bn_aggr(
                out=tiles[("mean_var", g)][:, t, :],
                in_=tiles[("stats", g)][:, t, :, :].rearrange("p h s -> p (h s)"),
            )

        def row_scalars(g):
            mean_var = tiles[("mean_var", g)]
            neg_mean = row_pool.tile([P, TILES], F32, name="neg_mean")
            var_eps = row_pool.tile([P, TILES], F32, name="var_eps")
            nc.vector.tensor_scalar(out=neg_mean[:], in0=mean_var[:, :, 0], scalar1=-1.0, scalar2=None, op0=ALU.mult)
            nc.vector.tensor_scalar(out=var_eps[:], in0=mean_var[:, :, 1], scalar1=LN_EPS, scalar2=None, op0=ALU.add)
            tiles[("neg_mean", g)] = neg_mean
            tiles[("var_eps", g)] = var_eps

        def inverse_std(g):
            rstd = row_pool.tile([P, TILES], F32, name="rstd")
            nc.gpsimd.tensor_tensor(out=rstd[:], in0=tiles[("var_eps", g)][:], in1=minus_half[:], op=ALU.pow)
            tiles[("rstd", g)] = rstd

        def scalar_bias(g):
            bias = row_pool.tile([P, TILES], F32, name="bias")
            nc.gpsimd.tensor_tensor(
                out=bias[:], in0=tiles[("neg_mean", g)][:], in1=tiles[("rstd", g)][:], op=ALU.mult
            )
            tiles[("bias", g)] = bias

        def xhat(g, engine):
            mine = [share[1:] for share in shares(g) if share[0] == engine]
            if mine and ("xhat", g) not in tiles:
                tiles[("xhat", g)] = work.tile([P, TILES, D], F32, name="xhat")
            for t, lo, hi in mine:
                dst = tiles[("xhat", g)][:, t, lo:hi]
                src = tiles[("x", g)][:, t, lo:hi]
                rstd = tiles[("rstd", g)][:, t : t + 1]
                if engine == "scalar":
                    nc.scalar.activation(
                        out=dst, in_=src, func=ACT.Identity, bias=tiles[("bias", g)][:, t : t + 1], scale=rstd
                    )
                else:
                    eng = nc.gpsimd if engine == "gpsimd" else nc.vector
                    eng.tensor_scalar(
                        out=dst, in0=src, scalar1=tiles[("neg_mean", g)][:, t : t + 1], scalar2=rstd,
                        op0=ALU.add, op1=ALU.mult,
                    )

        def turn(g, j):
            if j == 0:
                tiles[("planes", g)] = work.tile([P, PASSES, PACK, GROUP], BF16, name="planes")
            bank = turn_banks.tile([P, GROUP], F32, tag="bank", name="bank")
            for t in range(TILES):
                nc.tensor.transpose(
                    out=bank[:, t * P : (t + 1) * P],
                    in_=tiles[("xhat", g)][:, t, j * P : (j + 1) * P],
                    identity=ident[:],
                )
            nc.scalar.activation(
                out=tiles[("planes", g)][:, j // PACK, j % PACK, :], in_=bank[:], func=ACT.Identity,
                bias=param(COL_B + j), scale=param(COL_G + j),
            )

        def regroup(g, c):
            if c == 0:
                tiles[("words", g)] = work.tile([P, PASSES, GROUP, PACK], BF16, align_bytes=64, name="words")
            nc.vector.tensor_copy(
                out=tiles[("words", g)][:, c].rearrange("p (w i) t -> p w t i", i=4),
                in_=tiles[("planes", g)][:, c].rearrange("p t (w i) -> p w t i", i=4),
            )

        def quantise(g):
            codes = work.tile([P, PASSES * GROUP], U32, align_bytes=64, name="codes")
            scales = work.tile([P, PASSES * GROUP], U8, align_bytes=64, name="scales")
            nc.vector.quantize_mx(
                out=codes[:].bitcast(FP8X4), scales=scales[:],
                in_=tiles[("words", g)][:].rearrange("p c n t -> p (c n t)"),
            )
            tiles[("codes", g)] = codes
            tiles[("scales", g)] = scales

        def multiply(g):
            codes = tiles[("codes", g)]
            scales = tiles[("scales", g)]
            silu = work.tile([P, F // P, GROUP], F32, name="silu")
            tiles[("silu", g)] = silu
            accs = []
            for h in range(F // P):
                acc = mx_banks.tile([P, GROUP], F32, name="acc")
                accs.append(acc)
                for c in range(PASSES):
                    w0 = c * F + h * P
                    nc.tensor.matmul_mx(
                        out=acc[:],
                        lhsT=w_codes[:, w0 : w0 + P].bitcast(FP8X4),
                        lhsT_scale=w_scales[:, w0 : w0 + P],
                        rhs=codes[:, c * GROUP : (c + 1) * GROUP].bitcast(FP8X4),
                        rhs_scale=scales[:, c * GROUP : (c + 1) * GROUP],
                        start=(c == 0),
                        stop=(c == PASSES - 1),
                    )
            for h in range(F // P):
                nc.scalar.activation(
                    out=silu[:, h, :], in_=accs[h][:], func=ACT.Silu, bias=param(COL_BIAS + h), scale=1.0
                )

        def scale_offset(g):
            z = tiles[("silu", g)][:, 1, :]
            qk = work.tile([P, 2, GROUP], F32, name="qk")
            tiles[("qk", g)] = qk
            for i in range(2):
                nc.vector.tensor_scalar(
                    out=qk[:, i, :], in0=z,
                    scalar1=param(COL_GAMMA_BETA + 2 * i), scalar2=param(COL_GAMMA_BETA + 2 * i + 1),
                    op0=ALU.mult, op1=ALU.add,
                )

        def emit_out(g, i):
            src = tiles[("silu", g)][:, 0, :] if i == 0 else tiles[("qk", g)][:, i - 1, :]
            rows = slice(g * GROUP, (g + 1) * GROUP)
            bank = turn_banks.tile([P, GROUP], F32, tag="bank", name="out_bank")
            for t in range(TILES):
                nc.tensor.transpose(
                    out=bank[:, t * P : (t + 1) * P], in_=src[:, t * P : (t + 1) * P], identity=ident[:]
                )
            if i == 0:
                uv = store_pool.tile([P, 2, TILES, E], F32, name="uv")
                nc.scalar.copy(
                    out=uv[:].rearrange("p c t f -> p t c f"),
                    in_=bank[:].rearrange("p (t c f) -> p t c f", t=TILES, c=2),
                )
                for c in range(2):
                    nc.sync.dma_start(
                        out=outs[c][rows, :].rearrange("(p t) f -> p (t f)", t=TILES),
                        in_=uv[:, c].rearrange("p t f -> p (t f)"),
                    )
            else:
                q_or_k = store_pool.tile([P, TILES * S], F32, name="q_or_k", bufs=6)
                nc.scalar.copy(out=q_or_k[:], in_=bank[:])
                nc.sync.dma_start(
                    out=outs[1 + i][rows, :].rearrange("(p t) f -> p (t f)", t=TILES), in_=q_or_k[:]
                )

        for i in range(-STAT_AHEAD, GROUPS + 1):
            g_stat = i + STAT_AHEAD
            g_xhat = i + XHAT_AHEAD
            if i >= 0 and live(i + LOAD_AHEAD):
                load(i + LOAD_AHEAD)

            if live(g_xhat - 1):
                xhat(g_xhat - 1, "vector")
            if live(i):
                regroup(i, 0)
            if live(g_stat - 1):
                aggregate(g_stat - 1, TILES - 1)
            if live(i):
                regroup(i, 1)
            if live(i) and not live(g_stat):
                quantise(i)
            if live(i - 1):
                scale_offset(i - 1)
            if live(g_stat - 1):
                row_scalars(g_stat - 1)
            if live(i) and live(g_stat):
                quantise(i)

            if live(g_xhat):
                inverse_std(g_xhat)
                if any(share[0] == "scalar" for share in shares(g_xhat)):
                    scalar_bias(g_xhat)
                xhat(g_xhat, "gpsimd")
            if live(g_stat):
                stats_tile(g_stat, 0)
                for t in range(1, TILES):
                    stats_tile(g_stat, t)
                    aggregate(g_stat, t - 1)
            if g_stat == 0:
                prepare_params()
            if g_stat == 1:
                prepare_w()

            if live(i + 1):
                for j in range(K_BLOCKS):
                    turn(i + 1, j)
            if live(g_xhat):
                xhat(g_xhat, "scalar")
            if live(i):
                multiply(i)
            if live(i - 1):
                for k in range(3):
                    emit_out(i - 1, k)
